import numpy as np
import ml_dtypes


def mxq(x, axis, fmt="e4m3"):
    dtype, down = {"e4m3": (ml_dtypes.float8_e4m3fn, 7), "e5m2": (ml_dtypes.float8_e5m2, 14)}[fmt]
    v = np.moveaxis(np.asarray(x, np.float32).astype(ml_dtypes.bfloat16).astype(np.float64), axis, -1)
    blocks = v.reshape(v.shape[:-1] + (-1, 32))
    amax = np.abs(blocks).max(-1, keepdims=True)
    byte = np.maximum(np.where(amax > 0, np.frexp(amax)[1] - 1 + 127, 0) - down, 1)
    scale = np.exp2(byte - 127.0)
    codes = (blocks / scale).astype(np.float32).astype(dtype).astype(np.float64)
    return np.moveaxis((codes * scale).reshape(v.shape), -1, axis)


WIDE = False


def mx_kscale(k):
    if not WIDE:
        return np.ones(k)
    levels = np.array([10, -10, 5, -5, 0])
    a = np.random.permutation(np.resize(levels, k // 512 * 4)).reshape(k // 512, 4)
    idx = np.arange(k)
    return np.exp2(a[idx // 512, idx % 128 // 32])


BF16 = ml_dtypes.bfloat16


def bf(x):
    return np.asarray(x, np.float32).astype(BF16)


def f64(x):
    return np.asarray(x).astype(np.float64)


B, N, D = 32, 256, 512


def setup_inputs():
    s = mx_kscale(D)
    return {"panel_embeddings": bf(np.random.standard_normal((B, N, D)) * s),
            "W": bf(np.random.standard_normal((D, D)) * 4.0 / D / s[:, None] / s[None, :]),
            "b": bf(0.5 + 0.1 * np.random.standard_normal(1))}


def reference(panel_embeddings, W, b):
    xq = mxq(f64(panel_embeddings), 2, "e4m3")
    xw = xq @ mxq(f64(W), 0, "e4m3")
    scores = (mxq(xw, 2, "e4m3") @ xq.transpose(0, 2, 1)) + f64(b)
    n = panel_embeddings.shape[1]
    mask = ~np.eye(n, dtype=bool)
    return np.where(mask, scores, np.zeros_like(scores))

@@ -1,0 +1,192 @@
+from contextlib import ExitStack
+
+import concourse.mybir as mybir
+from concourse.masks import make_identity
+
+F32 = mybir.dt.float32
+BF16 = mybir.dt.bfloat16
+U32 = mybir.dt.uint32
+U8 = mybir.dt.uint8
+FP8X4 = mybir.dt.float8_e4m3fn_x4
+ADD = mybir.AluOpType.add
+MULT = mybir.AluOpType.mult
+
+P = 128
+B, N, D = 32, 256, 512
+FLOPS = 2 * B * N * D * D + 2 * B * N * N * D
+CH = 2
+NC = B // CH
+MANUAL = True
+
+
+def tile_readingorderhead_t_kernel(tc, panel_embeddings, W, b, out):
+    nc = tc.nc
+    x = panel_embeddings
+    with ExitStack() as ctx:
+        const = ctx.enter_context(tc.tile_pool(name="const", bufs=1))
+        xin = ctx.enter_context(tc.tile_pool(name="xin", bufs=1))
+        work = ctx.enter_context(tc.tile_pool(name="work", bufs=2))
+        codes = ctx.enter_context(tc.tile_pool(name="codes", bufs=4))
+        outp = ctx.enter_context(tc.tile_pool(name="outp", bufs=4))
+        psum = ctx.enter_context(tc.psum_pool(name="psum", bufs=2))
+        if MANUAL:
+            ctx.enter_context(tc.manual_schedule())
+
+        w_raw = const.tile([P, 4, D], BF16, name="w_raw")
+        nc.sync.dma_start(
+            out=w_raw[:].rearrange("p (u e) n -> p u (e n)", u=2),
+            in_=W.rearrange("(u p e) n -> p u (e n)", u=2, e=2),
+        )
+        bias_bf = const.tile([P, 1], BF16, name="bias_bf")
+        nc.scalar.dma_start(out=bias_bf[:], in_=b.partition_broadcast(P))
+        x_raw = []
+        for c in range(NC):
+            xr = xin.tile([P, CH * 2 * D], BF16, name="x_raw%d" % c)
+            nc.sync.dma_start(
+                out=xr[:].rearrange("p (b f) -> p b f", b=CH),
+                in_=x[CH * c : CH * (c + 1)].rearrange("b (p r) d -> p b (r d)", r=2),
+            )
+            x_raw.append(xr)
+
+        ident = const.tile([P, P], F32, name="ident")
+        make_identity(nc, ident[:])
+        mask = const.tile([P, 2 * N], F32, name="mask")
+        nc.vector.memset(mask[:], 1.0)
+        mask_v = mask[:].rearrange("p (r q s) -> p r q s", r=2, q=P, s=2)
+        for r in range(2):
+            nc.vector.tensor_scalar(
+                out=mask_v[:, r, :, r], in0=ident[:], scalar1=-1.0, scalar2=1.0, op0=MULT, op1=ADD
+            )
+        bias = const.tile([P, 1], F32, name="bias")
+
+        wg = const.tile([P, 4 * D], BF16, name="wg", align_bytes=64)
+        wg_v = wg[:].rearrange("p (o m t) -> p o m t", o=4, m=P, t=4)
+        w_v = w_raw[:].rearrange("p t (u m e) -> p u e m t", u=2, m=P, e=2)
+        for o in range(4):
+            src = w_v[:, o // 2, o % 2, :, :]
+            if o == 3:
+                nc.scalar.copy(out=wg_v[:, o, :, :], in_=src)
+            else:
+                nc.vector.tensor_copy(out=wg_v[:, o, :, :], in_=src)
+        wc = const.tile([P, D], U32, name="wc", align_bytes=64)
+        ws = const.tile([P, D], U8, name="ws", align_bytes=64)
+        nc.vector.quantize_mx(out=wc[:].bitcast(FP8X4), scales=ws[:], in_=wg[:])
+
+        xt_t, xg_t, xc_t, xs_t = {}, {}, {}, {}
+        xw_t, xwg_t, xwc_t, xws_t, sc_t = {}, {}, {}, {}, {}
+
+        def stage_t(c):
+            xr32 = x_raw[c][:].bitcast(F32)
+            for bb in range(CH):
+                xt = psum.tile([P, 4, P], F32, name="xt", tag="xt", bufs=2)
+                for s in range(4):
+                    lo = 512 * bb + 128 * s
+                    nc.tensor.transpose(xt[:, s, :], xr32[:, lo : lo + 128], ident[:])
+                xt_t[(c, bb)] = xt
+
+        def stage_cx(c):
+            xg = work.tile([P, CH * 4 * N], BF16, name="xg", tag="xg", align_bytes=64)
+            xg32 = xg[:].bitcast(F32)
+            for bb in range(CH):
+                dst = xg32[:, 512 * bb : 512 * (bb + 1)].rearrange("q (p s) -> q p s", s=4)
+                src = xt_t[(c, bb)][:].rearrange("q s p -> q p s")
+                if c == 0 and bb == 1:
+                    nc.vector.tensor_copy(out=dst, in_=src)
+                else:
+                    nc.scalar.copy(out=dst, in_=src)
+            xg_t[c] = xg
+
+        def stage_qx(c):
+            xc = codes.tile([P, CH * N], U32, name="xc", tag="xc", align_bytes=64)
+            xs = codes.tile([P, CH * N], U8, name="xs", tag="xs", align_bytes=64)
+            nc.vector.quantize_mx(out=xc[:].bitcast(FP8X4), scales=xs[:], in_=xg_t[c][:])
+            xc_t[c] = xc
+            xs_t[c] = xs
+
+        def stage_s1(c):
+            xc, xs = xc_t[c], xs_t[c]
+            for g in range(2 * CH):
+                xw = psum.tile([P, 4, P], F32, name="xw", tag="xw", bufs=4)
+                for t in range(4):
+                    nc.tensor.matmul_mx(
+                        out=xw[:, t, :],
+                        lhsT=wc[:, P * t : P * (t + 1)].bitcast(FP8X4),
+                        lhsT_scale=ws[:, P * t : P * (t + 1)],
+                        rhs=xc[:, P * g : P * (g + 1)].bitcast(FP8X4),
+                        rhs_scale=xs[:, P * g : P * (g + 1)],
+                        start=True,
+                        stop=True,
+                    )
+                xw_t[(c, g)] = xw
+
+        def stage_cw(c):
+            xwg = work.tile([P, CH * 4 * N], BF16, name="xwg", tag="xwg", align_bytes=64)
+            xwg_v = xwg[:].rearrange("p (b r m t) -> p b r m t", b=CH, r=2, m=P, t=4)
+            for g in range(2 * CH):
+                bb, a = g // 2, g % 2
+                dst = xwg_v[:, bb, :, 64 * a : 64 * (a + 1), :]
+                src = xw_t[(c, g)][:].rearrange("p t (m r) -> p r m t", r=2)
+                if g == 1 and c % 5 != 4:
+                    nc.vector.tensor_copy(out=dst, in_=src)
+                else:
+                    nc.scalar.copy(out=dst, in_=src)
+            xwg_t[c] = xwg
+
+        def stage_qw(c):
+            xwc = codes.tile([P, CH * N], U32, name="xwc", tag="xwc", bufs=2, align_bytes=64)
+            xws = codes.tile([P, CH * N], U8, name="xws", tag="xws", bufs=2, align_bytes=64)
+            nc.vector.quantize_mx(out=xwc[:].bitcast(FP8X4), scales=xws[:], in_=xwg_t[c][:])
+            xwc_t[c] = xwc
+            xws_t[c] = xws
+
+        def stage_s2(c):
+            xc, xs, xwc, xws = xc_t[c], xs_t[c], xwc_t[c], xws_t[c]
+            for bb in range(CH):
+                sc = psum.tile([P, 2, N], F32, name="sc", tag="sc", bufs=2)
+                for r in range(2):
+                    lo = N * bb + P * r
+                    nc.tensor.matmul_mx(
+                        out=sc[:, r, :],
+                        lhsT=xwc[:, lo : lo + P].bitcast(FP8X4),
+                        lhsT_scale=xws[:, lo : lo + P],
+                        rhs=xc[:, N * bb : N * (bb + 1)].bitcast(FP8X4),
+                        rhs_scale=xs[:, N * bb : N * (bb + 1)],
+                        start=True,
+                        stop=True,
+                    )
+                sc_t[(c, bb)] = sc
+
+        def stage_ex(c):
+            o = outp.tile([P, CH, 2 * N], F32, name="o", tag="o")
+            for bb in range(CH):
+                nc.vector.scalar_tensor_tensor(
+                    out=o[:, bb, :],
+                    in0=sc_t[(c, bb)][:].rearrange("p r j -> p (r j)"),
+                    scalar=bias[:, 0:1],
+                    in1=mask[:],
+                    op0=ADD,
+                    op1=MULT,
+                )
+            nc.sync.dma_start(
+                out=out[CH * c : CH * (c + 1)].rearrange("b (p r) j -> p b (r j)", r=2),
+                in_=o[:],
+            )
+
+        for c in range(-1, NC + 1):
+            if c + 1 < NC:
+                stage_t(c + 1)
+            if 0 <= c - 1:
+                stage_qw(c - 1)
+            if c + 1 < NC:
+                stage_cx(c + 1)
+            if 0 <= c < NC:
+                stage_s1(c)
+            if c + 1 < NC:
+                stage_qx(c + 1)
+            if 0 <= c < NC:
+                stage_cw(c)
+            if c == 0:
+                nc.vector.tensor_copy(out=bias[:], in_=bias_bf[:])
+            if 0 <= c - 1:
+                stage_s2(c - 1)
+                stage_ex(c - 1)

@@ -16,7 +16,7 @@ B, N, D = 32, 256, 512
 FLOPS = 2 * B * N * D * D + 2 * B * N * N * D
 CH = 2
 NC = B // CH
-MANUAL = True
+MANUAL = False
 
 
 def tile_readingorderhead_t_kernel(tc, panel_embeddings, W, b, out):

@@ -14,9 +14,18 @@ MULT = mybir.AluOpType.mult
 P = 128
 B, N, D = 32, 256, 512
 FLOPS = 2 * B * N * D * D + 2 * B * N * N * D
-CH = 2
-NC = B // CH
-MANUAL = False
+NC = B // 2
+MANUAL = True
+
+
+def cx_on_vector(b):
+    return b == 3
+
+
+def cw_on_vector(c, g):
+    if c < 2:
+        return g in (1, 3)
+    return c < 14 and g == 1 and c % 6 != 0
 
 
 def tile_readingorderhead_t_kernel(tc, panel_embeddings, W, b, out):
@@ -25,28 +34,34 @@ def tile_readingorderhead_t_kernel(tc, panel_embeddings, W, b, out):
     with ExitStack() as ctx:
         const = ctx.enter_context(tc.tile_pool(name="const", bufs=1))
         xin = ctx.enter_context(tc.tile_pool(name="xin", bufs=1))
-        work = ctx.enter_context(tc.tile_pool(name="work", bufs=2))
-        codes = ctx.enter_context(tc.tile_pool(name="codes", bufs=4))
+        work = ctx.enter_context(tc.tile_pool(name="work", bufs=4))
         outp = ctx.enter_context(tc.tile_pool(name="outp", bufs=4))
         psum = ctx.enter_context(tc.psum_pool(name="psum", bufs=2))
         if MANUAL:
             ctx.enter_context(tc.manual_schedule())
 
+        x_of = {}
+
+        def load_x(b0, nb):
+            xr = xin.tile([P, nb * 2 * D], BF16, name="x_raw%d" % b0)
+            nc.sync.dma_start(
+                out=xr[:].rearrange("p (b f) -> p b f", b=nb),
+                in_=x[b0 : b0 + nb].rearrange("b (p r) d -> p b (r d)", r=2),
+            )
+            for j in range(nb):
+                x_of[b0 + j] = (xr, j)
+
+        load_x(0, 1)
         w_raw = const.tile([P, 4, D], BF16, name="w_raw")
         nc.sync.dma_start(
             out=w_raw[:].rearrange("p (u e) n -> p u (e n)", u=2),
             in_=W.rearrange("(u p e) n -> p u (e n)", u=2, e=2),
         )
+        load_x(1, 1)
         bias_bf = const.tile([P, 1], BF16, name="bias_bf")
         nc.scalar.dma_start(out=bias_bf[:], in_=b.partition_broadcast(P))
-        x_raw = []
-        for c in range(NC):
-            xr = xin.tile([P, CH * 2 * D], BF16, name="x_raw%d" % c)
-            nc.sync.dma_start(
-                out=xr[:].rearrange("p (b f) -> p b f", b=CH),
-                in_=x[CH * c : CH * (c + 1)].rearrange("b (p r) d -> p b (r d)", r=2),
-            )
-            x_raw.append(xr)
+        for c in range(1, NC):
+            load_x(2 * c, 2)
 
         ident = const.tile([P, P], F32, name="ident")
         make_identity(nc, ident[:])
@@ -60,133 +75,198 @@ def tile_readingorderhead_t_kernel(tc, panel_embeddings, W, b, out):
         bias = const.tile([P, 1], F32, name="bias")
 
         wg = const.tile([P, 4 * D], BF16, name="wg", align_bytes=64)
-        wg_v = wg[:].rearrange("p (o m t) -> p o m t", o=4, m=P, t=4)
-        w_v = w_raw[:].rearrange("p t (u m e) -> p u e m t", u=2, m=P, e=2)
-        for o in range(4):
-            src = w_v[:, o // 2, o % 2, :, :]
-            if o == 3:
-                nc.scalar.copy(out=wg_v[:, o, :, :], in_=src)
-            else:
-                nc.vector.tensor_copy(out=wg_v[:, o, :, :], in_=src)
         wc = const.tile([P, D], U32, name="wc", align_bytes=64)
         ws = const.tile([P, D], U8, name="ws", align_bytes=64)
-        nc.vector.quantize_mx(out=wc[:].bitcast(FP8X4), scales=ws[:], in_=wg[:])
 
-        xt_t, xg_t, xc_t, xs_t = {}, {}, {}, {}
-        xw_t, xwg_t, xwc_t, xws_t, sc_t = {}, {}, {}, {}, {}
+        def w_regroup():
+            wg_v = wg[:].rearrange("p (o m t) -> p o m t", o=4, m=P, t=4)
+            w_v = w_raw[:].rearrange("p t (u m e) -> p u e m t", u=2, m=P, e=2)
+            for o in range(4):
+                src = w_v[:, o // 2, o % 2, :, :]
+                if o == 3:
+                    nc.scalar.copy(out=wg_v[:, o, :, :], in_=src)
+                else:
+                    nc.vector.tensor_copy(out=wg_v[:, o, :, :], in_=src)
 
-        def stage_t(c):
-            xr32 = x_raw[c][:].bitcast(F32)
-            for bb in range(CH):
+        def w_quantise():
+            nc.vector.quantize_mx(out=wc[:].bitcast(FP8X4), scales=ws[:], in_=wg[:])
+            nc.vector.tensor_copy(out=bias[:], in_=bias_bf[:])
+
+        xt_t, xg_of, xc_of, xw_t, xwg_of, xwc_of, sc_t, o_of = {}, {}, {}, {}, {}, {}, {}, {}
+
+        def ok(c):
+            return 0 <= c < NC
+
+        def copy_out(on_vector, dst, src):
+            if on_vector:
+                nc.vector.tensor_copy(out=dst, in_=src)
+            else:
+                nc.scalar.copy(out=dst, in_=src)
+
+        def tr(c):
+            if not ok(c):
+                return
+            for bb in (2 * c, 2 * c + 1):
+                xr, j = x_of[bb]
+                xr32 = xr[:].bitcast(F32)
                 xt = psum.tile([P, 4, P], F32, name="xt", tag="xt", bufs=2)
                 for s in range(4):
-                    lo = 512 * bb + 128 * s
+                    lo = 512 * j + 128 * s
                     nc.tensor.transpose(xt[:, s, :], xr32[:, lo : lo + 128], ident[:])
-                xt_t[(c, bb)] = xt
+                xt_t[bb] = xt
 
-        def stage_cx(c):
-            xg = work.tile([P, CH * 4 * N], BF16, name="xg", tag="xg", align_bytes=64)
-            xg32 = xg[:].bitcast(F32)
-            for bb in range(CH):
-                dst = xg32[:, 512 * bb : 512 * (bb + 1)].rearrange("q (p s) -> q p s", s=4)
-                src = xt_t[(c, bb)][:].rearrange("q s p -> q p s")
-                if c == 0 and bb == 1:
-                    nc.vector.tensor_copy(out=dst, in_=src)
-                else:
-                    nc.scalar.copy(out=dst, in_=src)
-            xg_t[c] = xg
+        def cx(c, j):
+            if not ok(c):
+                return
+            bb = 2 * c + j
+            if c == 0:
+                xg = work.tile([P, 4 * N], BF16, name="xg", tag="xg", align_bytes=64)
+                xg_of[bb] = (xg, 0)
+            elif j == 0:
+                xg = work.tile([P, 8 * N], BF16, name="xg", tag="xg", align_bytes=64)
+                xg_of[bb] = (xg, 0)
+                xg_of[bb + 1] = (xg, 1)
+            xg, k = xg_of[bb]
+            dst = xg[:].bitcast(F32)[:, 512 * k : 512 * (k + 1)].rearrange("q (p s) -> q p s", s=4)
+            copy_out(cx_on_vector(bb), dst, xt_t[bb][:].rearrange("q s p -> q p s"))
 
-        def stage_qx(c):
-            xc = codes.tile([P, CH * N], U32, name="xc", tag="xc", align_bytes=64)
-            xs = codes.tile([P, CH * N], U8, name="xs", tag="xs", align_bytes=64)
-            nc.vector.quantize_mx(out=xc[:].bitcast(FP8X4), scales=xs[:], in_=xg_t[c][:])
-            xc_t[c] = xc
-            xs_t[c] = xs
+        def quantise(src, nb, tag, bufs):
+            cod = work.tile([P, nb * N], U32, name=tag + "c", tag=tag + "c", bufs=bufs, align_bytes=64)
+            sca = work.tile([P, nb * N], U8, name=tag + "s", tag=tag + "s", bufs=bufs, align_bytes=64)
+            nc.vector.quantize_mx(out=cod[:].bitcast(FP8X4), scales=sca[:], in_=src[:])
+            return cod, sca
 
-        def stage_s1(c):
-            xc, xs = xc_t[c], xs_t[c]
-            for g in range(2 * CH):
-                xw = psum.tile([P, 4, P], F32, name="xw", tag="xw", bufs=4)
-                for t in range(4):
-                    nc.tensor.matmul_mx(
-                        out=xw[:, t, :],
-                        lhsT=wc[:, P * t : P * (t + 1)].bitcast(FP8X4),
-                        lhsT_scale=ws[:, P * t : P * (t + 1)],
-                        rhs=xc[:, P * g : P * (g + 1)].bitcast(FP8X4),
-                        rhs_scale=xs[:, P * g : P * (g + 1)],
-                        start=True,
-                        stop=True,
-                    )
-                xw_t[(c, g)] = xw
+        def qx(c):
+            if not ok(c):
+                return
+            if c == 0:
+                for bb in (0, 1):
+                    cod, sca = quantise(xg_of[bb][0], 1, "xq", 7)
+                    xc_of[bb] = (cod, sca, 0)
+            else:
+                cod, sca = quantise(xg_of[2 * c][0], 2, "xq", 7)
+                xc_of[2 * c] = (cod, sca, 0)
+                xc_of[2 * c + 1] = (cod, sca, 1)
 
-        def stage_cw(c):
-            xwg = work.tile([P, CH * 4 * N], BF16, name="xwg", tag="xwg", align_bytes=64)
-            xwg_v = xwg[:].rearrange("p (b r m t) -> p b r m t", b=CH, r=2, m=P, t=4)
-            for g in range(2 * CH):
-                bb, a = g // 2, g % 2
-                dst = xwg_v[:, bb, :, 64 * a : 64 * (a + 1), :]
-                src = xw_t[(c, g)][:].rearrange("p t (m r) -> p r m t", r=2)
-                if g == 1 and c % 5 != 4:
-                    nc.vector.tensor_copy(out=dst, in_=src)
-                else:
-                    nc.scalar.copy(out=dst, in_=src)
-            xwg_t[c] = xwg
+        def s1(c, g):
+            if not ok(c):
+                return
+            cod, sca, k = xc_of[2 * c + g // 2]
+            lo = N * k + P * (g % 2)
+            xw = psum.tile([P, 4, P], F32, name="xw", tag="xw", bufs=4)
+            for t in range(4):
+                nc.tensor.matmul_mx(
+                    out=xw[:, t, :],
+                    lhsT=wc[:, P * t : P * (t + 1)].bitcast(FP8X4),
+                    lhsT_scale=ws[:, P * t : P * (t + 1)],
+                    rhs=cod[:, lo : lo + P].bitcast(FP8X4),
+                    rhs_scale=sca[:, lo : lo + P],
+                    start=True,
+                    stop=True,
+                )
+            xw_t[(c, g)] = xw
 
-        def stage_qw(c):
-            xwc = codes.tile([P, CH * N], U32, name="xwc", tag="xwc", bufs=2, align_bytes=64)
-            xws = codes.tile([P, CH * N], U8, name="xws", tag="xws", bufs=2, align_bytes=64)
-            nc.vector.quantize_mx(out=xwc[:].bitcast(FP8X4), scales=xws[:], in_=xwg_t[c][:])
-            xwc_t[c] = xwc
-            xws_t[c] = xws
+        def cw(c, g):
+            if not ok(c):
+                return
+            bb, a = 2 * c + g // 2, g % 2
+            if c == NC - 1:
+                if a == 0:
+                    xwg = work.tile([P, 4 * N], BF16, name="xwg", tag="xwg", align_bytes=64)
+                    xwg_of[bb] = (xwg, 0, 1)
+            elif g == 0:
+                xwg = work.tile([P, 8 * N], BF16, name="xwg", tag="xwg", align_bytes=64)
+                xwg_of[bb] = (xwg, 0, 2)
+                xwg_of[bb + 1] = (xwg, 1, 2)
+            xwg, k, nb = xwg_of[bb]
+            xwg_v = xwg[:].rearrange("p (b r m t) -> p b r m t", b=nb, r=2, m=P, t=4)
+            dst = xwg_v[:, k, :, 64 * a : 64 * (a + 1), :]
+            copy_out(cw_on_vector(c, g), dst, xw_t[(c, g)][:].rearrange("p t (m r) -> p r m t", r=2))
 
-        def stage_s2(c):
-            xc, xs, xwc, xws = xc_t[c], xs_t[c], xwc_t[c], xws_t[c]
-            for bb in range(CH):
+        def qw_batch(bb):
+            cod, sca = quantise(xwg_of[bb][0], 1, "wq", 4)
+            xwc_of[bb] = (cod, sca, 0)
+
+        def qw(c):
+            if not ok(c):
+                return
+            cod, sca = quantise(xwg_of[2 * c][0], 2, "wq", 4)
+            xwc_of[2 * c] = (cod, sca, 0)
+            xwc_of[2 * c + 1] = (cod, sca, 1)
+
+        def s2(c):
+            if not ok(c):
+                return
+            for bb in (2 * c, 2 * c + 1):
+                xcod, xsca, k = xc_of[bb]
+                wcod, wsca, kw = xwc_of[bb]
                 sc = psum.tile([P, 2, N], F32, name="sc", tag="sc", bufs=2)
                 for r in range(2):
-                    lo = N * bb + P * r
+                    lo = N * kw + P * r
                     nc.tensor.matmul_mx(
                         out=sc[:, r, :],
-                        lhsT=xwc[:, lo : lo + P].bitcast(FP8X4),
-                        lhsT_scale=xws[:, lo : lo + P],
-                        rhs=xc[:, N * bb : N * (bb + 1)].bitcast(FP8X4),
-                        rhs_scale=xs[:, N * bb : N * (bb + 1)],
+                        lhsT=wcod[:, lo : lo + P].bitcast(FP8X4),
+                        lhsT_scale=wsca[:, lo : lo + P],
+                        rhs=xcod[:, N * k : N * (k + 1)].bitcast(FP8X4),
+                        rhs_scale=xsca[:, N * k : N * (k + 1)],
                         start=True,
                         stop=True,
                     )
-                sc_t[(c, bb)] = sc
+                sc_t[bb] = sc
 
-        def stage_ex(c):
-            o = outp.tile([P, CH, 2 * N], F32, name="o", tag="o")
-            for bb in range(CH):
-                nc.vector.scalar_tensor_tensor(
-                    out=o[:, bb, :],
-                    in0=sc_t[(c, bb)][:].rearrange("p r j -> p (r j)"),
-                    scalar=bias[:, 0:1],
-                    in1=mask[:],
-                    op0=ADD,
-                    op1=MULT,
-                )
+        def store(b0, nb, o):
             nc.sync.dma_start(
-                out=out[CH * c : CH * (c + 1)].rearrange("b (p r) j -> p b (r j)", r=2),
-                in_=o[:],
+                out=out[b0 : b0 + nb].rearrange("b (p r) j -> p b (r j)", r=2), in_=o[:]
             )
 
-        for c in range(-1, NC + 1):
-            if c + 1 < NC:
-                stage_t(c + 1)
-            if 0 <= c - 1:
-                stage_qw(c - 1)
-            if c + 1 < NC:
-                stage_cx(c + 1)
-            if 0 <= c < NC:
-                stage_s1(c)
-            if c + 1 < NC:
-                stage_qx(c + 1)
-            if 0 <= c < NC:
-                stage_cw(c)
-            if c == 0:
-                nc.vector.tensor_copy(out=bias[:], in_=bias_bf[:])
-            if 0 <= c - 1:
-                stage_s2(c - 1)
-                stage_ex(c - 1)
+        def ex(c, j):
+            if not ok(c):
+                return
+            bb = 2 * c + j
+            if c == NC - 1:
+                o = outp.tile([P, 1, 2 * N], F32, name="o", tag="o")
+                o_of[bb] = (o, 0)
+            elif j == 0:
+                o = outp.tile([P, 2, 2 * N], F32, name="o", tag="o")
+                o_of[bb] = (o, 0)
+                o_of[bb + 1] = (o, 1)
+            o, k = o_of[bb]
+            nc.vector.scalar_tensor_tensor(
+                out=o[:, k, :],
+                in0=sc_t[bb][:].rearrange("p r j -> p (r j)"),
+                scalar=bias[:, 0:1],
+                in1=mask[:],
+                op0=ADD,
+                op1=MULT,
+            )
+            if c == NC - 1:
+                store(bb, 1, o)
+            elif j == 1:
+                store(bb - 1, 2, o)
+
+        for i in range(-2, NC + 3):
+            s1(i, 0)
+            cw(i - 1, 3)
+            s1(i, 1)
+            if i == -1:
+                w_regroup()
+            cx(i + 1, 0)
+            s1(i, 2)
+            cx(i + 1, 1)
+            s1(i, 3)
+            if i - 1 == NC - 1:
+                qw_batch(B - 2)
+                ex(i - 2, 0)
+                qw_batch(B - 1)
+            else:
+                ex(i - 2, 0)
+                qw(i - 1)
+            ex(i - 2, 1)
+            if i == -1:
+                w_quantise()
+            tr(i + 2)
+            cw(i, 0)
+            s2(i - 1)
+            qx(i + 1)
+            cw(i, 1)
+            cw(i, 2)

@@ -16,6 +16,7 @@ B, N, D = 32, 256, 512
 FLOPS = 2 * B * N * D * D + 2 * B * N * N * D
 NC = B // 2
 MANUAL = True
+LOADS_AHEAD = 10
 
 
 def cx_on_vector(b):
@@ -35,7 +36,7 @@ def tile_readingorderhead_t_kernel(tc, panel_embeddings, W, b, out):
         const = ctx.enter_context(tc.tile_pool(name="const", bufs=1))
         xin = ctx.enter_context(tc.tile_pool(name="xin", bufs=1))
         work = ctx.enter_context(tc.tile_pool(name="work", bufs=4))
-        outp = ctx.enter_context(tc.tile_pool(name="outp", bufs=4))
+        outp = ctx.enter_context(tc.tile_pool(name="outp", bufs=8))
         psum = ctx.enter_context(tc.psum_pool(name="psum", bufs=2))
         if MANUAL:
             ctx.enter_context(tc.manual_schedule())
@@ -60,7 +61,7 @@ def tile_readingorderhead_t_kernel(tc, panel_embeddings, W, b, out):
         load_x(1, 1)
         bias_bf = const.tile([P, 1], BF16, name="bias_bf")
         nc.scalar.dma_start(out=bias_bf[:], in_=b.partition_broadcast(P))
-        for c in range(1, NC):
+        for c in range(1, LOADS_AHEAD):
             load_x(2 * c, 2)
 
         ident = const.tile([P, P], F32, name="ident")
@@ -243,6 +244,8 @@ def tile_readingorderhead_t_kernel(tc, panel_embeddings, W, b, out):
                 store(bb, 1, o)
             elif j == 1:
                 store(bb - 1, 2, o)
+                if c + LOADS_AHEAD < NC:
+                    load_x(2 * (c + LOADS_AHEAD), 2)
 
         for i in range(-2, NC + 3):
             s1(i, 0)

@@ -59,8 +59,11 @@ def tile_readingorderhead_t_kernel(tc, panel_embeddings, W, b, out):
             in_=W.rearrange("(u p e) n -> p u (e n)", u=2, e=2),
         )
         load_x(1, 1)
-        bias_bf = const.tile([P, 1], BF16, name="bias_bf")
-        nc.scalar.dma_start(out=bias_bf[:], in_=b.partition_broadcast(P))
+        b_row = const.tile([P, 32], BF16, name="b_row")
+        nc.vector.memset(b_row[:], 0.0)
+        nc.scalar.dma_start(out=b_row[0:1, 0:1], in_=b.unsqueeze(0))
+        ones = const.tile([P, P], BF16, name="ones")
+        nc.vector.memset(ones[:], 1.0)
         for c in range(1, LOADS_AHEAD):
             load_x(2 * c, 2)
 
@@ -91,7 +94,7 @@ def tile_readingorderhead_t_kernel(tc, panel_embeddings, W, b, out):
 
         def w_quantise():
             nc.vector.quantize_mx(out=wc[:].bitcast(FP8X4), scales=ws[:], in_=wg[:])
-            nc.vector.tensor_copy(out=bias[:], in_=bias_bf[:])
+            nc.vector.tensor_copy(out=bias[:], in_=bias_ps[0][:, 0:1])
 
         xt_t, xg_of, xc_of, xw_t, xwg_of, xwc_of, sc_t, o_of = {}, {}, {}, {}, {}, {}, {}, {}
 
@@ -104,10 +107,19 @@ def tile_readingorderhead_t_kernel(tc, panel_embeddings, W, b, out):
             else:
                 nc.scalar.copy(out=dst, in_=src)
 
+        bias_ps = []
+
+        def spread_bias():
+            bp = psum.tile([P, 32], F32, name="bp", tag="sc", bufs=2)
+            nc.tensor.matmul(out=bp[:], lhsT=ones[:], rhs=b_row[:], start=True, stop=True)
+            bias_ps.append(bp)
+
         def tr(c):
             if not ok(c):
                 return
             for bb in (2 * c, 2 * c + 1):
+                if bb == 1:
+                    spread_bias()
                 xr, j = x_of[bb]
                 xr32 = xr[:].bitcast(F32)
                 xt = psum.tile([P, 4, P], F32, name="xt", tag="xt", bufs=2)

from contextlib import ExitStack

import concourse.mybir as mybir
from concourse.masks import make_identity

F32 = mybir.dt.float32
BF16 = mybir.dt.bfloat16
U32 = mybir.dt.uint32
U8 = mybir.dt.uint8
FP8X4 = mybir.dt.float8_e4m3fn_x4
ADD = mybir.AluOpType.add
MULT = mybir.AluOpType.mult

P = 128
B, N, D = 32, 256, 512
FLOPS = 2 * B * N * D * D + 2 * B * N * N * D
NC = B // 2
MANUAL = True
LOADS_AHEAD = 10


def cx_on_vector(b):
    return b == 3


def cw_on_vector(c, g):
    if c < 2:
        return g in (1, 3)
    return c < 14 and g == 1 and c % 6 != 0


def tile_readingorderhead_t_kernel(tc, panel_embeddings, W, b, out):
    nc = tc.nc
    x = panel_embeddings
    with ExitStack() as ctx:
        const = ctx.enter_context(tc.tile_pool(name="const", bufs=1))
        xin = ctx.enter_context(tc.tile_pool(name="xin", bufs=1))
        work = ctx.enter_context(tc.tile_pool(name="work", bufs=4))
        outp = ctx.enter_context(tc.tile_pool(name="outp", bufs=8))
        psum = ctx.enter_context(tc.psum_pool(name="psum", bufs=2))
        if MANUAL:
            ctx.enter_context(tc.manual_schedule())

        x_of = {}

        def load_x(b0, nb):
            xr = xin.tile([P, nb * 2 * D], BF16, name="x_raw%d" % b0)
            nc.sync.dma_start(
                out=xr[:].rearrange("p (b f) -> p b f", b=nb),
                in_=x[b0 : b0 + nb].rearrange("b (p r) d -> p b (r d)", r=2),
            )
            for j in range(nb):
                x_of[b0 + j] = (xr, j)

        load_x(0, 1)
        w_raw = const.tile([P, 4, D], BF16, name="w_raw")
        nc.sync.dma_start(
            out=w_raw[:].rearrange("p (u e) n -> p u (e n)", u=2),
            in_=W.rearrange("(u p e) n -> p u (e n)", u=2, e=2),
        )
        load_x(1, 1)
        b_row = const.tile([P, 32], BF16, name="b_row")
        nc.vector.memset(b_row[:], 0.0)
        nc.scalar.dma_start(out=b_row[0:1, 0:1], in_=b.unsqueeze(0))
        ones = const.tile([P, P], BF16, name="ones")
        nc.vector.memset(ones[:], 1.0)
        for c in range(1, LOADS_AHEAD):
            load_x(2 * c, 2)

        ident = const.tile([P, P], F32, name="ident")
        make_identity(nc, ident[:])
        mask = const.tile([P, 2 * N], F32, name="mask")
        nc.vector.memset(mask[:], 1.0)
        mask_v = mask[:].rearrange("p (r q s) -> p r q s", r=2, q=P, s=2)
        for r in range(2):
            nc.vector.tensor_scalar(
                out=mask_v[:, r, :, r], in0=ident[:], scalar1=-1.0, scalar2=1.0, op0=MULT, op1=ADD
            )
        bias = const.tile([P, 1], F32, name="bias")

        wg = const.tile([P, 4 * D], BF16, name="wg", align_bytes=64)
        wc = const.tile([P, D], U32, name="wc", align_bytes=64)
        ws = const.tile([P, D], U8, name="ws", align_bytes=64)

        def w_regroup():
            wg_v = wg[:].rearrange("p (o m t) -> p o m t", o=4, m=P, t=4)
            w_v = w_raw[:].rearrange("p t (u m e) -> p u e m t", u=2, m=P, e=2)
            for o in range(4):
                src = w_v[:, o // 2, o % 2, :, :]
                if o == 3:
                    nc.scalar.copy(out=wg_v[:, o, :, :], in_=src)
                else:
                    nc.vector.tensor_copy(out=wg_v[:, o, :, :], in_=src)

        def w_quantise():
            nc.vector.quantize_mx(out=wc[:].bitcast(FP8X4), scales=ws[:], in_=wg[:])
            nc.vector.tensor_copy(out=bias[:], in_=bias_ps[0][:, 0:1])

        xt_t, xg_of, xc_of, xw_t, xwg_of, xwc_of, sc_t, o_of = {}, {}, {}, {}, {}, {}, {}, {}

        def ok(c):
            return 0 <= c < NC

        def copy_out(on_vector, dst, src):
            if on_vector:
                nc.vector.tensor_copy(out=dst, in_=src)
            else:
                nc.scalar.copy(out=dst, in_=src)

        bias_ps = []

        def spread_bias():
            bp = psum.tile([P, 32], F32, name="bp", tag="sc", bufs=2)
            nc.tensor.matmul(out=bp[:], lhsT=ones[:], rhs=b_row[:], start=True, stop=True)
            bias_ps.append(bp)

        def tr(c):
            if not ok(c):
                return
            for bb in (2 * c, 2 * c + 1):
                if bb == 1:
                    spread_bias()
                xr, j = x_of[bb]
                xr32 = xr[:].bitcast(F32)
                xt = psum.tile([P, 4, P], F32, name="xt", tag="xt", bufs=2)
                for s in range(4):
                    lo = 512 * j + 128 * s
                    nc.tensor.transpose(xt[:, s, :], xr32[:, lo : lo + 128], ident[:])
                xt_t[bb] = xt

        def cx(c, j):
            if not ok(c):
                return
            bb = 2 * c + j
            if c == 0:
                xg = work.tile([P, 4 * N], BF16, name="xg", tag="xg", align_bytes=64)
                xg_of[bb] = (xg, 0)
            elif j == 0:
                xg = work.tile([P, 8 * N], BF16, name="xg", tag="xg", align_bytes=64)
                xg_of[bb] = (xg, 0)
                xg_of[bb + 1] = (xg, 1)
            xg, k = xg_of[bb]
            dst = xg[:].bitcast(F32)[:, 512 * k : 512 * (k + 1)].rearrange("q (p s) -> q p s", s=4)
            copy_out(cx_on_vector(bb), dst, xt_t[bb][:].rearrange("q s p -> q p s"))

        def quantise(src, nb, tag, bufs):
            cod = work.tile([P, nb * N], U32, name=tag + "c", tag=tag + "c", bufs=bufs, align_bytes=64)
            sca = work.tile([P, nb * N], U8, name=tag + "s", tag=tag + "s", bufs=bufs, align_bytes=64)
            nc.vector.quantize_mx(out=cod[:].bitcast(FP8X4), scales=sca[:], in_=src[:])
            return cod, sca

        def qx(c):
            if not ok(c):
                return
            if c == 0:
                for bb in (0, 1):
                    cod, sca = quantise(xg_of[bb][0], 1, "xq", 7)
                    xc_of[bb] = (cod, sca, 0)
            else:
                cod, sca = quantise(xg_of[2 * c][0], 2, "xq", 7)
                xc_of[2 * c] = (cod, sca, 0)
                xc_of[2 * c + 1] = (cod, sca, 1)

        def s1(c, g):
            if not ok(c):
                return
            cod, sca, k = xc_of[2 * c + g // 2]
            lo = N * k + P * (g % 2)
            xw = psum.tile([P, 4, P], F32, name="xw", tag="xw", bufs=4)
            for t in range(4):
                nc.tensor.matmul_mx(
                    out=xw[:, t, :],
                    lhsT=wc[:, P * t : P * (t + 1)].bitcast(FP8X4),
                    lhsT_scale=ws[:, P * t : P * (t + 1)],
                    rhs=cod[:, lo : lo + P].bitcast(FP8X4),
                    rhs_scale=sca[:, lo : lo + P],
                    start=True,
                    stop=True,
                )
            xw_t[(c, g)] = xw

        def cw(c, g):
            if not ok(c):
                return
            bb, a = 2 * c + g // 2, g % 2
            if c == NC - 1:
                if a == 0:
                    xwg = work.tile([P, 4 * N], BF16, name="xwg", tag="xwg", align_bytes=64)
                    xwg_of[bb] = (xwg, 0, 1)
            elif g == 0:
                xwg = work.tile([P, 8 * N], BF16, name="xwg", tag="xwg", align_bytes=64)
                xwg_of[bb] = (xwg, 0, 2)
                xwg_of[bb + 1] = (xwg, 1, 2)
            xwg, k, nb = xwg_of[bb]
            xwg_v = xwg[:].rearrange("p (b r m t) -> p b r m t", b=nb, r=2, m=P, t=4)
            dst = xwg_v[:, k, :, 64 * a : 64 * (a + 1), :]
            copy_out(cw_on_vector(c, g), dst, xw_t[(c, g)][:].rearrange("p t (m r) -> p r m t", r=2))

        def qw_batch(bb):
            cod, sca = quantise(xwg_of[bb][0], 1, "wq", 4)
            xwc_of[bb] = (cod, sca, 0)

        def qw(c):
            if not ok(c):
                return
            cod, sca = quantise(xwg_of[2 * c][0], 2, "wq", 4)
            xwc_of[2 * c] = (cod, sca, 0)
            xwc_of[2 * c + 1] = (cod, sca, 1)

        def s2(c):
            if not ok(c):
                return
            for bb in (2 * c, 2 * c + 1):
                xcod, xsca, k = xc_of[bb]
                wcod, wsca, kw = xwc_of[bb]
                sc = psum.tile([P, 2, N], F32, name="sc", tag="sc", bufs=2)
                for r in range(2):
                    lo = N * kw + P * r
                    nc.tensor.matmul_mx(
                        out=sc[:, r, :],
                        lhsT=wcod[:, lo : lo + P].bitcast(FP8X4),
                        lhsT_scale=wsca[:, lo : lo + P],
                        rhs=xcod[:, N * k : N * (k + 1)].bitcast(FP8X4),
                        rhs_scale=xsca[:, N * k : N * (k + 1)],
                        start=True,
                        stop=True,
                    )
                sc_t[bb] = sc

        def store(b0, nb, o):
            nc.sync.dma_start(
                out=out[b0 : b0 + nb].rearrange("b (p r) j -> p b (r j)", r=2), in_=o[:]
            )

        def ex(c, j):
            if not ok(c):
                return
            bb = 2 * c + j
            if c == NC - 1:
                o = outp.tile([P, 1, 2 * N], F32, name="o", tag="o")
                o_of[bb] = (o, 0)
            elif j == 0:
                o = outp.tile([P, 2, 2 * N], F32, name="o", tag="o")
                o_of[bb] = (o, 0)
                o_of[bb + 1] = (o, 1)
            o, k = o_of[bb]
            nc.vector.scalar_tensor_tensor(
                out=o[:, k, :],
                in0=sc_t[bb][:].rearrange("p r j -> p (r j)"),
                scalar=bias[:, 0:1],
                in1=mask[:],
                op0=ADD,
                op1=MULT,
            )
            if c == NC - 1:
                store(bb, 1, o)
            elif j == 1:
                store(bb - 1, 2, o)
                if c + LOADS_AHEAD < NC:
                    load_x(2 * (c + LOADS_AHEAD), 2)

        for i in range(-2, NC + 3):
            s1(i, 0)
            cw(i - 1, 3)
            s1(i, 1)
            if i == -1:
                w_regroup()
            cx(i + 1, 0)
            s1(i, 2)
            cx(i + 1, 1)
            s1(i, 3)
            if i - 1 == NC - 1:
                qw_batch(B - 2)
                ex(i - 2, 0)
                qw_batch(B - 1)
            else:
                ex(i - 2, 0)
                qw(i - 1)
            ex(i - 2, 1)
            if i == -1:
                w_quantise()
            tr(i + 2)
            cw(i, 0)
            s2(i - 1)
            qx(i + 1)
            cw(i, 1)
            cw(i, 2)
